import numpy as np
import ml_dtypes


def mxq(x, axis, fmt="e4m3"):
    dtype, down = {"e4m3": (ml_dtypes.float8_e4m3fn, 7), "e5m2": (ml_dtypes.float8_e5m2, 14)}[fmt]
    v = np.moveaxis(np.asarray(x, np.float32).astype(ml_dtypes.bfloat16).astype(np.float64), axis, -1)
    blocks = v.reshape(v.shape[:-1] + (-1, 32))
    amax = np.abs(blocks).max(-1, keepdims=True)
    byte = np.maximum(np.where(amax > 0, np.frexp(amax)[1] - 1 + 127, 0) - down, 1)
    scale = np.exp2(byte - 127.0)
    codes = (blocks / scale).astype(np.float32).astype(dtype).astype(np.float64)
    return np.moveaxis((codes * scale).reshape(v.shape), -1, axis)


WIDE = False


def mx_kscale(k):
    if not WIDE:
        return np.ones(k)
    levels = np.array([10, -10, 5, -5, 0])
    a = np.random.permutation(np.resize(levels, k // 512 * 4)).reshape(k // 512, 4)
    idx = np.arange(k)
    return np.exp2(a[idx // 512, idx % 128 // 32])


BF16 = ml_dtypes.bfloat16


def bf(x):
    return np.asarray(x, np.float32).astype(BF16)


def f64(x):
    return np.asarray(x).astype(np.float64)


B, N, DIN, DH, DOUT, DIM = 8, 1024, 512, 128, 128, 512


def draw_ahat():
    g = np.random.standard_normal((N, N))
    u = np.random.standard_normal(N) * 0.5
    a = g - g.T + u[:, None] - u[None, :]
    m = (a > 0) + np.eye(N)
    dinv = 1.0 / np.sqrt(m.sum(0))
    return m * (dinv[:, None] * dinv[None, :])


def setup_inputs():
    s, t = mx_kscale(DIN), mx_kscale(N)
    r = np.random.standard_normal
    return {"x": bf((r((B, N, DIN)) * s / t[:, None]).reshape(B * N, DIN)),
            "ahat": bf(draw_ahat() * t[:, None]),
            "gcn1_w": bf(r((DIN, DH)) * 0.2 * np.sqrt(N / DIN) / s[:, None]),
            "gcn1_b": bf(r(DH) * 0.2)}


def reference(x, ahat, gcn1_w, gcn1_b):
    xb = f64(x).reshape(B, N, DIN)
    y = mxq(xb, 2, "e4m3") @ mxq(f64(gcn1_w), 0, "e4m3")
    h = (mxq(f64(ahat), 0, "e4m3").T @ mxq(y, 1, "e4m3")) + f64(gcn1_b)
    return np.maximum(h, 0.0)

@@ -1,0 +1,254 @@
+from contextlib import ExitStack
+
+import concourse.mybir as mybir
+from concourse.masks import make_identity
+
+F32 = mybir.dt.float32
+BF16 = mybir.dt.bfloat16
+U32 = mybir.dt.uint32
+U8 = mybir.dt.uint8
+FP8X4 = mybir.dt.float8_e4m3fn_x4
+
+P = 128
+PACK = 4
+K_PASS = P * PACK
+GRAPHS = 8
+NODES = 1024
+D_IN = 512
+D_OUT = 128
+NODE_PASSES = NODES // K_PASS
+PAIRS = GRAPHS // 2
+HALF = NODES // 2
+CHUNKS = 2 * PAIRS
+CHUNK_LAG = 3
+
+FLOPS = 2 * GRAPHS * NODES * D_IN * D_OUT + 2 * GRAPHS * NODES * NODES * D_OUT
+
+
+def tile_gcn_pb_kernel(tc, x, ahat, gcn1_w, gcn1_b, out):
+    nc = tc.nc
+    with ExitStack() as ctx:
+        keep = ctx.enter_context(tc.tile_pool(name="keep", bufs=1))
+        a_stage = ctx.enter_context(tc.tile_pool(name="a_stage", bufs=4))
+        x_stage = ctx.enter_context(tc.tile_pool(name="x_stage", bufs=4))
+        y_stage = ctx.enter_context(tc.tile_pool(name="y_stage", bufs=2))
+        o_stage = ctx.enter_context(tc.tile_pool(name="o_stage", bufs=4))
+        psum_t = ctx.enter_context(tc.psum_pool(name="psum_t", bufs=4))
+        psum_y = ctx.enter_context(tc.psum_pool(name="psum_y", bufs=2))
+        psum_o = ctx.enter_context(tc.psum_pool(name="psum_o", bufs=2))
+        ctx.enter_context(tc.manual_schedule())
+
+        x_sb = [keep.tile([P, NODE_PASSES, PACK, D_IN], BF16, name="x_sb%d" % g) for g in range(GRAPHS)]
+        a_raw = keep.tile([P, NODE_PASSES, PACK, NODES], BF16)
+        a_codes = keep.tile([P, NODE_PASSES, NODES], U32, align_bytes=64)
+        a_scales = keep.tile([P, NODE_PASSES, NODES], U8, align_bytes=64)
+        w_raw = keep.tile([P, PACK, D_OUT], BF16)
+        w_grouped = keep.tile([P, D_OUT, PACK], BF16, align_bytes=64)
+        w_codes = keep.tile([P, D_OUT], U32, align_bytes=64)
+        w_scales = keep.tile([P, D_OUT], U8, align_bytes=64)
+        identity = keep.tile([P, P], F32)
+        ones = keep.tile([P, P], BF16)
+        bias_rows = keep.tile([P, D_OUT], BF16)
+        bias_all = keep.tile([P, 4, D_OUT], F32)
+
+        make_identity(nc, identity[:])
+        nc.vector.memset(bias_rows[:], 0.0)
+        nc.vector.memset(ones[:], 1.0)
+
+        x_rows = x.rearrange("(g c p j) k -> g p c (j k)", g=GRAPHS, c=NODE_PASSES, p=P, j=PACK)
+        a_rows = ahat.rearrange("(c p j) n -> c p (j n)", c=NODE_PASSES, p=P, j=PACK)
+
+        def load_x(g, c_from, c_to):
+            nc.sync.dma_start(
+                out=x_sb[g][:, c_from:c_to].rearrange("p c j k -> p c (j k)"),
+                in_=x_rows[g][:, c_from:c_to, :],
+            )
+
+        def load_ahat(c):
+            nc.sync.dma_start(out=a_raw[:, c].rearrange("p j n -> p (j n)"), in_=a_rows[c])
+
+        load_x(0, 0, 1)
+        nc.sync.dma_start(
+            out=w_raw[:].rearrange("q (u e) f -> q u (e f)", u=2),
+            in_=gcn1_w.rearrange("(u q e) f -> q u (e f)", u=2, q=P, e=2),
+        )
+        nc.sync.dma_start(out=bias_rows[0:1, :], in_=gcn1_b.rearrange("(o f) -> o f", o=1))
+        load_x(0, 1, 2)
+        load_ahat(0)
+        load_x(1, 0, 2)
+        load_ahat(1)
+        for g in range(2, GRAPHS):
+            load_x(g, 0, 2)
+
+        xt_banks = {}
+        x_grouped = {}
+        x_codes = {}
+        x_scales = {}
+        y_banks = {}
+        y_grouped = {}
+        y_codes = {}
+        y_scales = {}
+        a_grouped = {}
+        o_banks = {}
+        o_tiles = {}
+
+        def transpose_x(g):
+            words = x_sb[g][:].bitcast(F32)
+            for bank in range(4):
+                xt = psum_t.tile([P, 2, 2, P], F32)
+                xt_banks[(g, bank)] = xt
+                for t in range(2):
+                    c, j = divmod(2 * bank + t, PACK)
+                    for u in range(2):
+                        nc.tensor.transpose(xt[:, t, u, :], words[:, c, j, u * P : (u + 1) * P], identity[:])
+
+        def copy_x(g, bank):
+            c, part = divmod(bank, 2)
+            if part == 0:
+                x_grouped[(g, c)] = x_stage.tile([P, PACK, P, PACK], BF16, name="x_grouped", align_bytes=64)
+            nc.scalar.copy(
+                out=x_grouped[(g, c)][:].bitcast(F32)[:, 2 * part : 2 * part + 2, :, :],
+                in_=xt_banks[(g, bank)][:].rearrange("q t u n -> q t n u"),
+            )
+
+        def quantise_x(g, c):
+            x_codes[(g, c)] = x_stage.tile([P, PACK * P], U32, name="x_codes", align_bytes=64)
+            x_scales[(g, c)] = x_stage.tile([P, PACK * P], U8, name="x_scales", align_bytes=64)
+            nc.vector.quantize_mx(
+                out=x_codes[(g, c)][:].bitcast(FP8X4),
+                scales=x_scales[(g, c)][:],
+                in_=x_grouped[(g, c)][:].rearrange("q j n k -> q (j n k)"),
+            )
+
+        def project(g, c):
+            y_bank = psum_y.tile([P, PACK, D_OUT], F32)
+            y_banks[(g, c)] = y_bank
+            for j in range(PACK):
+                nodes = slice(j * P, (j + 1) * P)
+                nc.tensor.matmul_mx(
+                    out=y_bank[:, j, :],
+                    lhsT=x_codes[(g, c)][:, nodes].bitcast(FP8X4),
+                    lhsT_scale=x_scales[(g, c)][:, nodes],
+                    rhs=w_codes[:].bitcast(FP8X4),
+                    rhs_scale=w_scales[:],
+                    start=True,
+                    stop=True,
+                )
+
+        def copy_y(g, c):
+            pair, b = divmod(g, 2)
+            if b == 0 and c == 0:
+                y_grouped[pair] = y_stage.tile([P, NODE_PASSES, 2, D_OUT, PACK], BF16, name="y_grouped", align_bytes=64)
+            nc.scalar.copy(out=y_grouped[pair][:, c, b, :, :], in_=y_banks[(g, c)][:].rearrange("p j f -> p f j"))
+
+        def quantise_y(pair):
+            y_codes[pair] = y_stage.tile([P, NODE_PASSES, 2 * D_OUT], U32, name="y_codes", align_bytes=64)
+            y_scales[pair] = y_stage.tile([P, NODE_PASSES, 2 * D_OUT], U8, name="y_scales", align_bytes=64)
+            nc.vector.quantize_mx(
+                out=y_codes[pair][:].rearrange("p c n -> p (c n)").bitcast(FP8X4),
+                scales=y_scales[pair][:].rearrange("p c n -> p (c n)"),
+                in_=y_grouped[pair][:].rearrange("p c b f j -> p (c b f j)"),
+            )
+
+        def regroup_ahat(copy, c, half):
+            a_grouped[(c, half)] = a_stage.tile([P, HALF, PACK], BF16, name="a_grouped", align_bytes=64)
+            copy(
+                out=a_grouped[(c, half)][:].rearrange("p (w i) j -> p w j i", i=4),
+                in_=a_raw[:, c, :, half * HALF : (half + 1) * HALF].rearrange("p j (w i) -> p w j i", i=4),
+            )
+
+        def quantise_ahat(c, half):
+            cols = slice(half * HALF, (half + 1) * HALF)
+            nc.vector.quantize_mx(
+                out=a_codes[:, c, cols].bitcast(FP8X4),
+                scales=a_scales[:, c, cols],
+                in_=a_grouped[(c, half)][:].rearrange("p n j -> p (n j)"),
+            )
+
+        def aggregate(chunk):
+            pair, half = divmod(chunk, 2)
+            for bank in range(2):
+                o_bank = psum_o.tile([P, 2, 2 * D_OUT], F32)
+                o_banks[(chunk, bank)] = o_bank
+                for t in range(2):
+                    first = half * HALF + (2 * bank + t) * P
+                    for c in range(NODE_PASSES):
+                        nc.tensor.matmul_mx(
+                            out=o_bank[:, t, :],
+                            lhsT=a_codes[:, c, first : first + P].bitcast(FP8X4),
+                            lhsT_scale=a_scales[:, c, first : first + P],
+                            rhs=y_codes[pair][:, c, :].bitcast(FP8X4),
+                            rhs_scale=y_scales[pair][:, c, :],
+                            start=(c == 0),
+                            stop=(c == NODE_PASSES - 1),
+                        )
+
+        def add_bias(chunk, bank):
+            if bank == 0:
+                o_tiles[chunk] = o_stage.tile([P, 2, 4, D_OUT], F32, name="o_tile")
+            nc.vector.tensor_tensor(
+                out=o_tiles[chunk][:, :, 2 * bank : 2 * bank + 2, :].rearrange("p b t f -> p t b f"),
+                in0=o_banks[(chunk, bank)][:].rearrange("p t (b f) -> p t b f", b=2),
+                in1=bias_all[:].rearrange("p (t b) f -> p t b f", t=2),
+                op=mybir.AluOpType.add,
+            )
+
+        def relu_and_store(chunk):
+            pair, half = divmod(chunk, 2)
+            flat = o_tiles[chunk][:].rearrange("p b t f -> p (b t f)")
+            nc.vector.tensor_scalar_max(out=flat, in0=flat, scalar1=0.0)
+            for b in range(2):
+                rows = out[2 * pair + b].rearrange("(t p) f -> p t f", p=P)
+                nc.sync.dma_start(out=rows[:, 4 * half : 4 * half + 4, :], in_=o_tiles[chunk][:, b, :, :])
+
+        transpose_x(0)
+        bias_bank = psum_o.tile([P, 2, 2 * D_OUT], F32, tag="o_bank")
+        nc.tensor.matmul(out=bias_bank[:, 0, 0:D_OUT], lhsT=ones[:], rhs=bias_rows[:], start=True, stop=True)
+        nc.vector.tensor_copy(out=w_grouped[:], in_=w_raw[:].rearrange("q t f -> q f t"))
+        nc.vector.tensor_copy(
+            out=bias_all[:], in_=bias_bank[:, 0, 0:D_OUT].unsqueeze(1).to_broadcast([P, 4, D_OUT])
+        )
+        nc.vector.quantize_mx(
+            out=w_codes[:].bitcast(FP8X4), scales=w_scales[:], in_=w_grouped[:].rearrange("q f t -> q (f t)")
+        )
+
+        for n in range(CHUNKS + CHUNK_LAG + 1):
+            chunk = n - CHUNK_LAG
+            has_x = n < GRAPHS
+            has_y = 1 <= n <= GRAPHS
+            has_a = 1 <= n <= NODE_PASSES
+            has_chunk = 0 <= chunk < CHUNKS
+
+            if has_chunk and chunk % 2 == 0:
+                quantise_y(chunk // 2)
+            if 0 <= chunk - 1 < CHUNKS:
+                relu_and_store(chunk - 1)
+            if has_x:
+                copy_x(n, 0)
+                copy_x(n, 1)
+            if has_a:
+                quantise_ahat(n - 1, 0)
+            if has_x:
+                quantise_x(n, 0)
+                copy_x(n, 2)
+                copy_x(n, 3)
+            if has_y:
+                project(n - 1, 0)
+                project(n - 1, 1)
+            if has_chunk:
+                aggregate(chunk)
+            if n + 1 < GRAPHS:
+                transpose_x(n + 1)
+            if has_y:
+                copy_y(n - 1, 0)
+                copy_y(n - 1, 1)
+            if has_chunk:
+                add_bias(chunk, 0)
+                add_bias(chunk, 1)
+            if has_a:
+                quantise_ahat(n - 1, 1)
+            if has_x:
+                quantise_x(n, 1)
+            if n < NODE_PASSES:
+                regroup_ahat(nc.vector.tensor_copy, n, 0)
+                regroup_ahat(nc.scalar.copy, n, 1)

@@ -50,10 +50,12 @@ def tile_gcn_pb_kernel(tc, x, ahat, gcn1_w, gcn1_b, out):
         ones = keep.tile([P, P], BF16)
         bias_rows = keep.tile([P, D_OUT], BF16)
         bias_all = keep.tile([P, 4, D_OUT], F32)
+        warm = keep.tile([P, 1], F32)
 
         make_identity(nc, identity[:])
         nc.vector.memset(bias_rows[:], 0.0)
         nc.vector.memset(ones[:], 1.0)
+        nc.scalar.activation(out=warm[:], in_=ones[:, 0:1], func=mybir.ActivationFunctionType.Relu)
 
         x_rows = x.rearrange("(g c p j) k -> g p c (j k)", g=GRAPHS, c=NODE_PASSES, p=P, j=PACK)
         a_rows = ahat.rearrange("(c p j) n -> c p (j n)", c=NODE_PASSES, p=P, j=PACK)
@@ -74,11 +76,10 @@ def tile_gcn_pb_kernel(tc, x, ahat, gcn1_w, gcn1_b, out):
         )
         nc.sync.dma_start(out=bias_rows[0:1, :], in_=gcn1_b.rearrange("(o f) -> o f", o=1))
         load_x(0, 1, 2)
-        load_ahat(0)
-        load_x(1, 0, 2)
-        load_ahat(1)
-        for g in range(2, GRAPHS):
-            load_x(g, 0, 2)
+        for g in range(1, GRAPHS):
+            load_x(g, 0, NODE_PASSES)
+            if g - 1 < NODE_PASSES:
+                load_ahat(g - 1)
 
         xt_banks = {}
         x_grouped = {}
@@ -120,26 +121,28 @@ def tile_gcn_pb_kernel(tc, x, ahat, gcn1_w, gcn1_b, out):
                 in_=x_grouped[(g, c)][:].rearrange("q j n k -> q (j n k)"),
             )
 
-        def project(g, c):
-            y_bank = psum_y.tile([P, PACK, D_OUT], F32)
-            y_banks[(g, c)] = y_bank
-            for j in range(PACK):
-                nodes = slice(j * P, (j + 1) * P)
-                nc.tensor.matmul_mx(
-                    out=y_bank[:, j, :],
-                    lhsT=x_codes[(g, c)][:, nodes].bitcast(FP8X4),
-                    lhsT_scale=x_scales[(g, c)][:, nodes],
-                    rhs=w_codes[:].bitcast(FP8X4),
-                    rhs_scale=w_scales[:],
-                    start=True,
-                    stop=True,
-                )
+        def project(g):
+            for c in range(NODE_PASSES):
+                y_bank = psum_y.tile([P, PACK, D_OUT], F32)
+                y_banks[(g, c)] = y_bank
+                for j in range(PACK):
+                    nodes = slice(j * P, (j + 1) * P)
+                    nc.tensor.matmul_mx(
+                        out=y_bank[:, j, :],
+                        lhsT=x_codes[(g, c)][:, nodes].bitcast(FP8X4),
+                        lhsT_scale=x_scales[(g, c)][:, nodes],
+                        rhs=w_codes[:].bitcast(FP8X4),
+                        rhs_scale=w_scales[:],
+                        start=True,
+                        stop=True,
+                    )
 
-        def copy_y(g, c):
+        def copy_y(g):
             pair, b = divmod(g, 2)
-            if b == 0 and c == 0:
+            if b == 0:
                 y_grouped[pair] = y_stage.tile([P, NODE_PASSES, 2, D_OUT, PACK], BF16, name="y_grouped", align_bytes=64)
-            nc.scalar.copy(out=y_grouped[pair][:, c, b, :, :], in_=y_banks[(g, c)][:].rearrange("p j f -> p f j"))
+            for c in range(NODE_PASSES):
+                nc.scalar.copy(out=y_grouped[pair][:, c, b, :, :], in_=y_banks[(g, c)][:].rearrange("p j f -> p f j"))
 
         def quantise_y(pair):
             y_codes[pair] = y_stage.tile([P, NODE_PASSES, 2 * D_OUT], U32, name="y_codes", align_bytes=64)
@@ -150,12 +153,13 @@ def tile_gcn_pb_kernel(tc, x, ahat, gcn1_w, gcn1_b, out):
                 in_=y_grouped[pair][:].rearrange("p c b f j -> p (c b f j)"),
             )
 
-        def regroup_ahat(copy, c, half):
-            a_grouped[(c, half)] = a_stage.tile([P, HALF, PACK], BF16, name="a_grouped", align_bytes=64)
-            copy(
-                out=a_grouped[(c, half)][:].rearrange("p (w i) j -> p w j i", i=4),
-                in_=a_raw[:, c, :, half * HALF : (half + 1) * HALF].rearrange("p j (w i) -> p w j i", i=4),
-            )
+        def regroup_ahat(c):
+            for half in range(2):
+                a_grouped[(c, half)] = a_stage.tile([P, HALF, PACK], BF16, name="a_grouped", align_bytes=64)
+                nc.vector.tensor_copy(
+                    out=a_grouped[(c, half)][:].rearrange("p (w i) j -> p w j i", i=4),
+                    in_=a_raw[:, c, :, half * HALF : (half + 1) * HALF].rearrange("p j (w i) -> p w j i", i=4),
+                )
 
         def quantise_ahat(c, half):
             cols = slice(half * HALF, (half + 1) * HALF)
@@ -185,70 +189,84 @@ def tile_gcn_pb_kernel(tc, x, ahat, gcn1_w, gcn1_b, out):
 
         def add_bias(chunk, bank):
             if bank == 0:
-                o_tiles[chunk] = o_stage.tile([P, 2, 4, D_OUT], F32, name="o_tile")
+                o_tiles[chunk] = o_stage.tile([P, 2, 2, 2, D_OUT], F32, name="o_tile")
             nc.vector.tensor_tensor(
-                out=o_tiles[chunk][:, :, 2 * bank : 2 * bank + 2, :].rearrange("p b t f -> p t b f"),
-                in0=o_banks[(chunk, bank)][:].rearrange("p t (b f) -> p t b f", b=2),
-                in1=bias_all[:].rearrange("p (t b) f -> p t b f", t=2),
+                out=o_tiles[chunk][:, bank].rearrange("p t b f -> p (t b f)"),
+                in0=o_banks[(chunk, bank)][:].rearrange("p t n -> p (t n)"),
+                in1=bias_all[:].rearrange("p r f -> p (r f)"),
                 op=mybir.AluOpType.add,
             )
 
-        def relu_and_store(chunk):
+        def store(chunk, bank_from, bank_to):
             pair, half = divmod(chunk, 2)
-            flat = o_tiles[chunk][:].rearrange("p b t f -> p (b t f)")
-            nc.vector.tensor_scalar_max(out=flat, in0=flat, scalar1=0.0)
             for b in range(2):
                 rows = out[2 * pair + b].rearrange("(t p) f -> p t f", p=P)
-                nc.sync.dma_start(out=rows[:, 4 * half : 4 * half + 4, :], in_=o_tiles[chunk][:, b, :, :])
+                nc.sync.dma_start(
+                    out=rows[:, 4 * half + 2 * bank_from : 4 * half + 2 * bank_to, :],
+                    in_=o_tiles[chunk][:, bank_from:bank_to, :, b, :].rearrange("p k t f -> p (k t) f"),
+                )
+
+        def relu_on_vector(chunk):
+            flat = o_tiles[chunk][:].rearrange("p k t b f -> p (k t b f)")
+            nc.vector.tensor_scalar_max(out=flat, in0=flat, scalar1=0.0)
+            store(chunk, 0, 2)
+
+        def relu_on_scalar(chunk, bank):
+            part = o_tiles[chunk][:, bank].rearrange("p t b f -> p (t b f)")
+            nc.scalar.activation(out=part, in_=part, func=mybir.ActivationFunctionType.Relu)
+            store(chunk, bank, bank + 1)
 
         transpose_x(0)
         bias_bank = psum_o.tile([P, 2, 2 * D_OUT], F32, tag="o_bank")
         nc.tensor.matmul(out=bias_bank[:, 0, 0:D_OUT], lhsT=ones[:], rhs=bias_rows[:], start=True, stop=True)
         nc.vector.tensor_copy(out=w_grouped[:], in_=w_raw[:].rearrange("q t f -> q f t"))
-        nc.vector.tensor_copy(
-            out=bias_all[:], in_=bias_bank[:, 0, 0:D_OUT].unsqueeze(1).to_broadcast([P, 4, D_OUT])
-        )
         nc.vector.quantize_mx(
             out=w_codes[:].bitcast(FP8X4), scales=w_scales[:], in_=w_grouped[:].rearrange("q f t -> q (f t)")
         )
 
-        for n in range(CHUNKS + CHUNK_LAG + 1):
+        for n in range(GRAPHS):
             chunk = n - CHUNK_LAG
-            has_x = n < GRAPHS
-            has_y = 1 <= n <= GRAPHS
-            has_a = 1 <= n <= NODE_PASSES
-            has_chunk = 0 <= chunk < CHUNKS
-
-            if has_chunk and chunk % 2 == 0:
+            quantise_a = 0 <= n - 2 < NODE_PASSES
+            if chunk >= 0 and chunk % 2 == 0:
                 quantise_y(chunk // 2)
-            if 0 <= chunk - 1 < CHUNKS:
-                relu_and_store(chunk - 1)
-            if has_x:
-                copy_x(n, 0)
-                copy_x(n, 1)
-            if has_a:
-                quantise_ahat(n - 1, 0)
-            if has_x:
-                quantise_x(n, 0)
-                copy_x(n, 2)
-                copy_x(n, 3)
-            if has_y:
-                project(n - 1, 0)
-                project(n - 1, 1)
-            if has_chunk:
+            copy_x(n, 0)
+            copy_x(n, 1)
+            if quantise_a:
+                quantise_ahat(n - 2, 0)
+            quantise_x(n, 0)
+            copy_x(n, 2)
+            copy_x(n, 3)
+            if chunk >= 1:
+                relu_on_vector(chunk - 1)
+            if n >= 1:
+                project(n - 1)
+            if chunk >= 0:
                 aggregate(chunk)
             if n + 1 < GRAPHS:
                 transpose_x(n + 1)
-            if has_y:
-                copy_y(n - 1, 0)
-                copy_y(n - 1, 1)
-            if has_chunk:
+            if n >= 1:
+                copy_y(n - 1)
+            if quantise_a:
+                quantise_ahat(n - 2, 1)
+            quantise_x(n, 1)
+            if chunk >= 0:
                 add_bias(chunk, 0)
                 add_bias(chunk, 1)
-            if has_a:
-                quantise_ahat(n - 1, 1)
-            if has_x:
-                quantise_x(n, 1)
-            if n < NODE_PASSES:
-                regroup_ahat(nc.vector.tensor_copy, n, 0)
-                regroup_ahat(nc.scalar.copy, n, 1)
+            if n == 0:
+                nc.vector.tensor_copy(
+                    out=bias_all[:], in_=bias_bank[:, 0, 0:D_OUT].unsqueeze(1).to_broadcast([P, 4, D_OUT])
+                )
+            if 0 <= n - 1 < NODE_PASSES:
+                regroup_ahat(n - 1)
+
+        project(GRAPHS - 1)
+        copy_y(GRAPHS - 1)
+        quantise_y(PAIRS - 1)
+        first_left = GRAPHS - CHUNK_LAG
+        for bank in range(2):
+            relu_on_scalar(first_left - 1, bank)
+        for chunk in range(first_left, CHUNKS):
+            aggregate(chunk)
+            for bank in range(2):
+                add_bias(chunk, bank)
+                relu_on_scalar(chunk, bank)

@@ -33,9 +33,8 @@ def tile_gcn_pb_kernel(tc, x, ahat, gcn1_w, gcn1_b, out):
         x_stage = ctx.enter_context(tc.tile_pool(name="x_stage", bufs=4))
         y_stage = ctx.enter_context(tc.tile_pool(name="y_stage", bufs=2))
         o_stage = ctx.enter_context(tc.tile_pool(name="o_stage", bufs=4))
-        psum_t = ctx.enter_context(tc.psum_pool(name="psum_t", bufs=4))
         psum_y = ctx.enter_context(tc.psum_pool(name="psum_y", bufs=2))
-        psum_o = ctx.enter_context(tc.psum_pool(name="psum_o", bufs=2))
+        psum_work = ctx.enter_context(tc.psum_pool(name="psum_work", bufs=6))
         ctx.enter_context(tc.manual_schedule())
 
         x_sb = [keep.tile([P, NODE_PASSES, PACK, D_IN], BF16, name="x_sb%d" % g) for g in range(GRAPHS)]
@@ -77,9 +76,9 @@ def tile_gcn_pb_kernel(tc, x, ahat, gcn1_w, gcn1_b, out):
         nc.sync.dma_start(out=bias_rows[0:1, :], in_=gcn1_b.rearrange("(o f) -> o f", o=1))
         load_x(0, 1, 2)
         for g in range(1, GRAPHS):
-            load_x(g, 0, NODE_PASSES)
             if g - 1 < NODE_PASSES:
                 load_ahat(g - 1)
+            load_x(g, 0, NODE_PASSES)
 
         xt_banks = {}
         x_grouped = {}
@@ -96,7 +95,7 @@ def tile_gcn_pb_kernel(tc, x, ahat, gcn1_w, gcn1_b, out):
         def transpose_x(g):
             words = x_sb[g][:].bitcast(F32)
             for bank in range(4):
-                xt = psum_t.tile([P, 2, 2, P], F32)
+                xt = psum_work.tile([P, 2, 2, P], F32, tag="bank")
                 xt_banks[(g, bank)] = xt
                 for t in range(2):
                     c, j = divmod(2 * bank + t, PACK)
@@ -155,10 +154,10 @@ def tile_gcn_pb_kernel(tc, x, ahat, gcn1_w, gcn1_b, out):
 
         def regroup_ahat(c):
             for half in range(2):
-                a_grouped[(c, half)] = a_stage.tile([P, HALF, PACK], BF16, name="a_grouped", align_bytes=64)
+                a_grouped[(c, half)] = a_stage.tile([P, 4, P, PACK], BF16, name="a_grouped", align_bytes=64)
                 nc.vector.tensor_copy(
-                    out=a_grouped[(c, half)][:].rearrange("p (w i) j -> p w j i", i=4),
-                    in_=a_raw[:, c, :, half * HALF : (half + 1) * HALF].rearrange("p j (w i) -> p w j i", i=4),
+                    out=a_grouped[(c, half)][:].rearrange("p r m j -> p m j r"),
+                    in_=a_raw[:, c, :, half * HALF : (half + 1) * HALF].rearrange("p j (m r) -> p m j r", r=4),
                 )
 
         def quantise_ahat(c, half):
@@ -166,13 +165,13 @@ def tile_gcn_pb_kernel(tc, x, ahat, gcn1_w, gcn1_b, out):
             nc.vector.quantize_mx(
                 out=a_codes[:, c, cols].bitcast(FP8X4),
                 scales=a_scales[:, c, cols],
-                in_=a_grouped[(c, half)][:].rearrange("p n j -> p (n j)"),
+                in_=a_grouped[(c, half)][:].rearrange("p r m j -> p (r m j)"),
             )
 
         def aggregate(chunk):
             pair, half = divmod(chunk, 2)
             for bank in range(2):
-                o_bank = psum_o.tile([P, 2, 2 * D_OUT], F32)
+                o_bank = psum_work.tile([P, 2, 2 * D_OUT], F32, tag="bank")
                 o_banks[(chunk, bank)] = o_bank
                 for t in range(2):
                     first = half * HALF + (2 * bank + t) * P
@@ -189,35 +188,32 @@ def tile_gcn_pb_kernel(tc, x, ahat, gcn1_w, gcn1_b, out):
 
         def add_bias(chunk, bank):
             if bank == 0:
-                o_tiles[chunk] = o_stage.tile([P, 2, 2, 2, D_OUT], F32, name="o_tile")
+                o_tiles[chunk] = o_stage.tile([P, 2, 4, D_OUT], F32, name="o_tile")
             nc.vector.tensor_tensor(
-                out=o_tiles[chunk][:, bank].rearrange("p t b f -> p (t b f)"),
-                in0=o_banks[(chunk, bank)][:].rearrange("p t n -> p (t n)"),
-                in1=bias_all[:].rearrange("p r f -> p (r f)"),
+                out=o_tiles[chunk][:, :, 2 * bank : 2 * bank + 2, :].rearrange("p b t f -> p t b f"),
+                in0=o_banks[(chunk, bank)][:].rearrange("p t (b f) -> p t b f", b=2),
+                in1=bias_all[:].rearrange("p (t b) f -> p t b f", t=2),
                 op=mybir.AluOpType.add,
             )
 
-        def store(chunk, bank_from, bank_to):
+        def store(chunk, b):
             pair, half = divmod(chunk, 2)
-            for b in range(2):
-                rows = out[2 * pair + b].rearrange("(t p) f -> p t f", p=P)
-                nc.sync.dma_start(
-                    out=rows[:, 4 * half + 2 * bank_from : 4 * half + 2 * bank_to, :],
-                    in_=o_tiles[chunk][:, bank_from:bank_to, :, b, :].rearrange("p k t f -> p (k t) f"),
-                )
+            rows = out[2 * pair + b].rearrange("(h m r) f -> h m (r f)", h=2, r=4)
+            nc.sync.dma_start(out=rows[half], in_=o_tiles[chunk][:, b].rearrange("p r f -> p (r f)"))
 
         def relu_on_vector(chunk):
-            flat = o_tiles[chunk][:].rearrange("p k t b f -> p (k t b f)")
+            flat = o_tiles[chunk][:].rearrange("p b r f -> p (b r f)")
             nc.vector.tensor_scalar_max(out=flat, in0=flat, scalar1=0.0)
-            store(chunk, 0, 2)
+            store(chunk, 0)
+            store(chunk, 1)
 
-        def relu_on_scalar(chunk, bank):
-            part = o_tiles[chunk][:, bank].rearrange("p t b f -> p (t b f)")
+        def relu_on_scalar(chunk, b):
+            part = o_tiles[chunk][:, b].rearrange("p r f -> p (r f)")
             nc.scalar.activation(out=part, in_=part, func=mybir.ActivationFunctionType.Relu)
-            store(chunk, bank, bank + 1)
+            store(chunk, b)
 
         transpose_x(0)
-        bias_bank = psum_o.tile([P, 2, 2 * D_OUT], F32, tag="o_bank")
+        bias_bank = psum_work.tile([P, 2, 2 * D_OUT], F32, tag="bank")
         nc.tensor.matmul(out=bias_bank[:, 0, 0:D_OUT], lhsT=ones[:], rhs=bias_rows[:], start=True, stop=True)
         nc.vector.tensor_copy(out=w_grouped[:], in_=w_raw[:].rearrange("q t f -> q f t"))
         nc.vector.quantize_mx(
@@ -226,13 +222,13 @@ def tile_gcn_pb_kernel(tc, x, ahat, gcn1_w, gcn1_b, out):
 
         for n in range(GRAPHS):
             chunk = n - CHUNK_LAG
-            quantise_a = 0 <= n - 2 < NODE_PASSES
+            quantise_a = 0 <= n - 1 < NODE_PASSES
             if chunk >= 0 and chunk % 2 == 0:
                 quantise_y(chunk // 2)
             copy_x(n, 0)
             copy_x(n, 1)
             if quantise_a:
-                quantise_ahat(n - 2, 0)
+                quantise_ahat(n - 1, 0)
             quantise_x(n, 0)
             copy_x(n, 2)
             copy_x(n, 3)
@@ -247,7 +243,7 @@ def tile_gcn_pb_kernel(tc, x, ahat, gcn1_w, gcn1_b, out):
             if n >= 1:
                 copy_y(n - 1)
             if quantise_a:
-                quantise_ahat(n - 2, 1)
+                quantise_ahat(n - 1, 1)
             quantise_x(n, 1)
             if chunk >= 0:
                 add_bias(chunk, 0)
@@ -256,17 +252,18 @@ def tile_gcn_pb_kernel(tc, x, ahat, gcn1_w, gcn1_b, out):
                 nc.vector.tensor_copy(
                     out=bias_all[:], in_=bias_bank[:, 0, 0:D_OUT].unsqueeze(1).to_broadcast([P, 4, D_OUT])
                 )
-            if 0 <= n - 1 < NODE_PASSES:
-                regroup_ahat(n - 1)
+            if n < NODE_PASSES:
+                regroup_ahat(n)
 
         project(GRAPHS - 1)
         copy_y(GRAPHS - 1)
         quantise_y(PAIRS - 1)
         first_left = GRAPHS - CHUNK_LAG
-        for bank in range(2):
-            relu_on_scalar(first_left - 1, bank)
+        for b in range(2):
+            relu_on_scalar(first_left - 1, b)
         for chunk in range(first_left, CHUNKS):
             aggregate(chunk)
-            for bank in range(2):
-                add_bias(chunk, bank)
-                relu_on_scalar(chunk, bank)
+            add_bias(chunk, 0)
+            add_bias(chunk, 1)
+            for b in range(2):
+                relu_on_scalar(chunk, b)

@@ -59,26 +59,28 @@ def tile_gcn_pb_kernel(tc, x, ahat, gcn1_w, gcn1_b, out):
         x_rows = x.rearrange("(g c p j) k -> g p c (j k)", g=GRAPHS, c=NODE_PASSES, p=P, j=PACK)
         a_rows = ahat.rearrange("(c p j) n -> c p (j n)", c=NODE_PASSES, p=P, j=PACK)
 
-        def load_x(g, c_from, c_to):
-            nc.sync.dma_start(
-                out=x_sb[g][:, c_from:c_to].rearrange("p c j k -> p c (j k)"),
-                in_=x_rows[g][:, c_from:c_to, :],
-            )
+        def load_x(g, c):
+            nc.sync.dma_start(out=x_sb[g][:, c].rearrange("p j k -> p (j k)"), in_=x_rows[g][:, c, :])
 
         def load_ahat(c):
             nc.sync.dma_start(out=a_raw[:, c].rearrange("p j n -> p (j n)"), in_=a_rows[c])
 
-        load_x(0, 0, 1)
-        nc.sync.dma_start(
-            out=w_raw[:].rearrange("q (u e) f -> q u (e f)", u=2),
-            in_=gcn1_w.rearrange("(u q e) f -> q u (e f)", u=2, q=P, e=2),
-        )
-        nc.sync.dma_start(out=bias_rows[0:1, :], in_=gcn1_b.rearrange("(o f) -> o f", o=1))
-        load_x(0, 1, 2)
-        for g in range(1, GRAPHS):
-            if g - 1 < NODE_PASSES:
-                load_ahat(g - 1)
-            load_x(g, 0, NODE_PASSES)
+        def load_weights():
+            nc.sync.dma_start(
+                out=w_raw[:].rearrange("q (u e) f -> q u (e f)", u=2),
+                in_=gcn1_w.rearrange("(u q e) f -> q u (e f)", u=2, q=P, e=2),
+            )
+            nc.sync.dma_start(out=bias_rows[0:1, :], in_=gcn1_b.rearrange("(o f) -> o f", o=1))
+
+        for g in range(GRAPHS):
+            for c in range(NODE_PASSES):
+                load_x(g, c)
+                if (g, c) == (0, 0):
+                    load_weights()
+                if (g, c) == (0, 1):
+                    load_ahat(0)
+                if (g, c) == (2, 0):
+                    load_ahat(1)
 
         xt_banks = {}
         x_grouped = {}
@@ -143,13 +145,14 @@ def tile_gcn_pb_kernel(tc, x, ahat, gcn1_w, gcn1_b, out):
             for c in range(NODE_PASSES):
                 nc.scalar.copy(out=y_grouped[pair][:, c, b, :, :], in_=y_banks[(g, c)][:].rearrange("p j f -> p f j"))
 
-        def quantise_y(pair):
-            y_codes[pair] = y_stage.tile([P, NODE_PASSES, 2 * D_OUT], U32, name="y_codes", align_bytes=64)
-            y_scales[pair] = y_stage.tile([P, NODE_PASSES, 2 * D_OUT], U8, name="y_scales", align_bytes=64)
+        def quantise_y(pair, c):
+            if c == 0:
+                y_codes[pair] = y_stage.tile([P, NODE_PASSES, 2 * D_OUT], U32, name="y_codes", align_bytes=64)
+                y_scales[pair] = y_stage.tile([P, NODE_PASSES, 2 * D_OUT], U8, name="y_scales", align_bytes=64)
             nc.vector.quantize_mx(
-                out=y_codes[pair][:].rearrange("p c n -> p (c n)").bitcast(FP8X4),
-                scales=y_scales[pair][:].rearrange("p c n -> p (c n)"),
-                in_=y_grouped[pair][:].rearrange("p c b f j -> p (c b f j)"),
+                out=y_codes[pair][:, c, :].bitcast(FP8X4),
+                scales=y_scales[pair][:, c, :],
+                in_=y_grouped[pair][:, c].rearrange("p b f j -> p (b f j)"),
             )
 
         def regroup_ahat(c):
@@ -224,7 +227,8 @@ def tile_gcn_pb_kernel(tc, x, ahat, gcn1_w, gcn1_b, out):
             chunk = n - CHUNK_LAG
             quantise_a = 0 <= n - 1 < NODE_PASSES
             if chunk >= 0 and chunk % 2 == 0:
-                quantise_y(chunk // 2)
+                quantise_y(chunk // 2, 0)
+                quantise_y(chunk // 2, 1)
             copy_x(n, 0)
             copy_x(n, 1)
             if quantise_a:
@@ -257,7 +261,8 @@ def tile_gcn_pb_kernel(tc, x, ahat, gcn1_w, gcn1_b, out):
 
         project(GRAPHS - 1)
         copy_y(GRAPHS - 1)
-        quantise_y(PAIRS - 1)
+        quantise_y(PAIRS - 1, 0)
+        quantise_y(PAIRS - 1, 1)
         first_left = GRAPHS - CHUNK_LAG
         for b in range(2):
             relu_on_scalar(first_left - 1, b)

@@ -17,9 +17,11 @@ NODES = 1024
 D_IN = 512
 D_OUT = 128
 NODE_PASSES = NODES // K_PASS
-PAIRS = GRAPHS // 2
+GROUPS = [(0, 1), (2, 3), (4, 5), (6,), (7,)]
 HALF = NODES // 2
-CHUNKS = 2 * PAIRS
+CHUNKS = [(q, half) for q in range(len(GROUPS)) for half in range(2)]
+TILES = 4
+PIECES = [(0, 0), (1, 0), (0, 1), (1, 1)]
 CHUNK_LAG = 3
 
 FLOPS = 2 * GRAPHS * NODES * D_IN * D_OUT + 2 * GRAPHS * NODES * NODES * D_OUT
@@ -32,13 +34,13 @@ def tile_gcn_pb_kernel(tc, x, ahat, gcn1_w, gcn1_b, out):
         a_stage = ctx.enter_context(tc.tile_pool(name="a_stage", bufs=4))
         x_stage = ctx.enter_context(tc.tile_pool(name="x_stage", bufs=4))
         y_stage = ctx.enter_context(tc.tile_pool(name="y_stage", bufs=2))
-        o_stage = ctx.enter_context(tc.tile_pool(name="o_stage", bufs=4))
+        o_stage = ctx.enter_context(tc.tile_pool(name="o_stage", bufs=len(CHUNKS)))
         psum_y = ctx.enter_context(tc.psum_pool(name="psum_y", bufs=2))
         psum_work = ctx.enter_context(tc.psum_pool(name="psum_work", bufs=6))
         ctx.enter_context(tc.manual_schedule())
 
         x_sb = [keep.tile([P, NODE_PASSES, PACK, D_IN], BF16, name="x_sb%d" % g) for g in range(GRAPHS)]
-        a_raw = keep.tile([P, NODE_PASSES, PACK, NODES], BF16)
+        a_raw = [keep.tile([P, PACK, HALF], BF16, name="a_raw%d" % i) for i in range(len(PIECES))]
         a_codes = keep.tile([P, NODE_PASSES, NODES], U32, align_bytes=64)
         a_scales = keep.tile([P, NODE_PASSES, NODES], U8, align_bytes=64)
         w_raw = keep.tile([P, PACK, D_OUT], BF16)
@@ -48,7 +50,7 @@ def tile_gcn_pb_kernel(tc, x, ahat, gcn1_w, gcn1_b, out):
         identity = keep.tile([P, P], F32)
         ones = keep.tile([P, P], BF16)
         bias_rows = keep.tile([P, D_OUT], BF16)
-        bias_all = keep.tile([P, 4, D_OUT], F32)
+        bias_all = keep.tile([P, D_OUT], F32)
         warm = keep.tile([P, 1], F32)
 
         make_identity(nc, identity[:])
@@ -57,13 +59,15 @@ def tile_gcn_pb_kernel(tc, x, ahat, gcn1_w, gcn1_b, out):
         nc.scalar.activation(out=warm[:], in_=ones[:, 0:1], func=mybir.ActivationFunctionType.Relu)
 
         x_rows = x.rearrange("(g c p j) k -> g p c (j k)", g=GRAPHS, c=NODE_PASSES, p=P, j=PACK)
-        a_rows = ahat.rearrange("(c p j) n -> c p (j n)", c=NODE_PASSES, p=P, j=PACK)
+        a_rows = ahat.rearrange("(c p j) n -> c p j n", c=NODE_PASSES, p=P, j=PACK)
 
         def load_x(g, c):
             nc.sync.dma_start(out=x_sb[g][:, c].rearrange("p j k -> p (j k)"), in_=x_rows[g][:, c, :])
 
-        def load_ahat(c):
-            nc.sync.dma_start(out=a_raw[:, c].rearrange("p j n -> p (j n)"), in_=a_rows[c])
+        def load_ahat(piece):
+            c, half = PIECES[piece]
+            cols = slice(half * HALF, (half + 1) * HALF)
+            nc.sync.dma_start(out=a_raw[piece][:], in_=a_rows[c][:, :, cols])
 
         def load_weights():
             nc.sync.dma_start(
@@ -73,14 +77,12 @@ def tile_gcn_pb_kernel(tc, x, ahat, gcn1_w, gcn1_b, out):
             nc.sync.dma_start(out=bias_rows[0:1, :], in_=gcn1_b.rearrange("(o f) -> o f", o=1))
 
         for g in range(GRAPHS):
+            if g < len(PIECES):
+                load_ahat(g)
             for c in range(NODE_PASSES):
                 load_x(g, c)
                 if (g, c) == (0, 0):
                     load_weights()
-                if (g, c) == (0, 1):
-                    load_ahat(0)
-                if (g, c) == (2, 0):
-                    load_ahat(1)
 
         xt_banks = {}
         x_grouped = {}
@@ -139,69 +141,73 @@ def tile_gcn_pb_kernel(tc, x, ahat, gcn1_w, gcn1_b, out):
                     )
 
         def copy_y(g):
-            pair, b = divmod(g, 2)
+            q = [g in group for group in GROUPS].index(True)
+            size, b = len(GROUPS[q]), GROUPS[q].index(g)
             if b == 0:
-                y_grouped[pair] = y_stage.tile([P, NODE_PASSES, 2, D_OUT, PACK], BF16, name="y_grouped", align_bytes=64)
+                y_grouped[q] = y_stage.tile([P, NODE_PASSES, size, D_OUT, PACK], BF16, name="y_grouped", align_bytes=64)
             for c in range(NODE_PASSES):
-                nc.scalar.copy(out=y_grouped[pair][:, c, b, :, :], in_=y_banks[(g, c)][:].rearrange("p j f -> p f j"))
+                nc.scalar.copy(out=y_grouped[q][:, c, b, :, :], in_=y_banks[(g, c)][:].rearrange("p j f -> p f j"))
 
-        def quantise_y(pair, c):
-            if c == 0:
-                y_codes[pair] = y_stage.tile([P, NODE_PASSES, 2 * D_OUT], U32, name="y_codes", align_bytes=64)
-                y_scales[pair] = y_stage.tile([P, NODE_PASSES, 2 * D_OUT], U8, name="y_scales", align_bytes=64)
+        def quantise_y(q):
+            size = len(GROUPS[q])
+            y_codes[q] = y_stage.tile([P, NODE_PASSES, size * D_OUT], U32, name="y_codes", align_bytes=64)
+            y_scales[q] = y_stage.tile([P, NODE_PASSES, size * D_OUT], U8, name="y_scales", align_bytes=64)
             nc.vector.quantize_mx(
-                out=y_codes[pair][:, c, :].bitcast(FP8X4),
-                scales=y_scales[pair][:, c, :],
-                in_=y_grouped[pair][:, c].rearrange("p b f j -> p (b f j)"),
+                out=y_codes[q][:].rearrange("p c n -> p (c n)").bitcast(FP8X4),
+                scales=y_scales[q][:].rearrange("p c n -> p (c n)"),
+                in_=y_grouped[q][:].rearrange("p c b f j -> p (c b f j)"),
             )
 
-        def regroup_ahat(c):
-            for half in range(2):
-                a_grouped[(c, half)] = a_stage.tile([P, 4, P, PACK], BF16, name="a_grouped", align_bytes=64)
-                nc.vector.tensor_copy(
-                    out=a_grouped[(c, half)][:].rearrange("p r m j -> p m j r"),
-                    in_=a_raw[:, c, :, half * HALF : (half + 1) * HALF].rearrange("p j (m r) -> p m j r", r=4),
-                )
+        def regroup_ahat(piece):
+            a_grouped[piece] = a_stage.tile([P, 4, P, PACK], BF16, name="a_grouped", align_bytes=64)
+            nc.vector.tensor_copy(
+                out=a_grouped[piece][:].rearrange("p r m j -> p m j r"),
+                in_=a_raw[piece][:].rearrange("p j (m r) -> p m j r", r=4),
+            )
 
-        def quantise_ahat(c, half):
+        def quantise_ahat(piece):
+            c, half = PIECES[piece]
             cols = slice(half * HALF, (half + 1) * HALF)
             nc.vector.quantize_mx(
                 out=a_codes[:, c, cols].bitcast(FP8X4),
                 scales=a_scales[:, c, cols],
-                in_=a_grouped[(c, half)][:].rearrange("p r m j -> p (r m j)"),
+                in_=a_grouped[piece][:].rearrange("p r m j -> p (r m j)"),
             )
 
         def aggregate(chunk):
-            pair, half = divmod(chunk, 2)
-            for bank in range(2):
-                o_bank = psum_work.tile([P, 2, 2 * D_OUT], F32, tag="bank")
+            q, half = CHUNKS[chunk]
+            size = len(GROUPS[q])
+            for bank in range(size):
+                o_bank = psum_work.tile([P, TILES // size, size * D_OUT], F32, tag="bank")
                 o_banks[(chunk, bank)] = o_bank
-                for t in range(2):
-                    first = half * HALF + (2 * bank + t) * P
+                for t in range(TILES // size):
+                    first = half * HALF + (bank * TILES // size + t) * P
                     for c in range(NODE_PASSES):
                         nc.tensor.matmul_mx(
                             out=o_bank[:, t, :],
                             lhsT=a_codes[:, c, first : first + P].bitcast(FP8X4),
                             lhsT_scale=a_scales[:, c, first : first + P],
-                            rhs=y_codes[pair][:, c, :].bitcast(FP8X4),
-                            rhs_scale=y_scales[pair][:, c, :],
+                            rhs=y_codes[q][:, c, :].bitcast(FP8X4),
+                            rhs_scale=y_scales[q][:, c, :],
                             start=(c == 0),
                             stop=(c == NODE_PASSES - 1),
                         )
 
         def add_bias(chunk, bank):
+            size = len(GROUPS[CHUNKS[chunk][0]])
             if bank == 0:
-                o_tiles[chunk] = o_stage.tile([P, 2, 4, D_OUT], F32, name="o_tile")
+                o_tiles[chunk] = o_stage.tile([P, size, TILES, D_OUT], F32, name="o_tile")
+            first = bank * TILES // size
             nc.vector.tensor_tensor(
-                out=o_tiles[chunk][:, :, 2 * bank : 2 * bank + 2, :].rearrange("p b t f -> p t b f"),
-                in0=o_banks[(chunk, bank)][:].rearrange("p t (b f) -> p t b f", b=2),
-                in1=bias_all[:].rearrange("p (t b) f -> p t b f", t=2),
+                out=o_tiles[chunk][:, :, first : first + TILES // size, :].rearrange("p b t f -> p t b f"),
+                in0=o_banks[(chunk, bank)][:].rearrange("p t (b f) -> p t b f", b=size),
+                in1=bias_all[:].unsqueeze(1).unsqueeze(1).to_broadcast([P, TILES // size, size, D_OUT]),
                 op=mybir.AluOpType.add,
             )
 
         def store(chunk, b):
-            pair, half = divmod(chunk, 2)
-            rows = out[2 * pair + b].rearrange("(h m r) f -> h m (r f)", h=2, r=4)
+            q, half = CHUNKS[chunk]
+            rows = out[GROUPS[q][b]].rearrange("(h m r) f -> h m (r f)", h=2, r=4)
             nc.sync.dma_start(out=rows[half], in_=o_tiles[chunk][:, b].rearrange("p r f -> p (r f)"))
 
         def relu_on_vector(chunk):
@@ -215,6 +221,7 @@ def tile_gcn_pb_kernel(tc, x, ahat, gcn1_w, gcn1_b, out):
             nc.scalar.activation(out=part, in_=part, func=mybir.ActivationFunctionType.Relu)
             store(chunk, b)
 
+        regroup_ahat(0)
         transpose_x(0)
         bias_bank = psum_work.tile([P, 2, 2 * D_OUT], F32, tag="bank")
         nc.tensor.matmul(out=bias_bank[:, 0, 0:D_OUT], lhsT=ones[:], rhs=bias_rows[:], start=True, stop=True)
@@ -225,15 +232,16 @@ def tile_gcn_pb_kernel(tc, x, ahat, gcn1_w, gcn1_b, out):
 
         for n in range(GRAPHS):
             chunk = n - CHUNK_LAG
-            quantise_a = 0 <= n - 1 < NODE_PASSES
+            quantise_a = 0 <= n - 1 < len(PIECES)
             if chunk >= 0 and chunk % 2 == 0:
-                quantise_y(chunk // 2, 0)
-                quantise_y(chunk // 2, 1)
+                quantise_y(chunk // 2)
             copy_x(n, 0)
             copy_x(n, 1)
             if quantise_a:
-                quantise_ahat(n - 1, 0)
+                quantise_ahat(n - 1)
             quantise_x(n, 0)
+            if n + 1 < len(PIECES):
+                regroup_ahat(n + 1)
             copy_x(n, 2)
             copy_x(n, 3)
             if chunk >= 1:
@@ -246,29 +254,33 @@ def tile_gcn_pb_kernel(tc, x, ahat, gcn1_w, gcn1_b, out):
                 transpose_x(n + 1)
             if n >= 1:
                 copy_y(n - 1)
-            if quantise_a:
-                quantise_ahat(n - 1, 1)
             quantise_x(n, 1)
+            if n == GRAPHS - 1:
+                quantise_y(3)
             if chunk >= 0:
                 add_bias(chunk, 0)
                 add_bias(chunk, 1)
             if n == 0:
-                nc.vector.tensor_copy(
-                    out=bias_all[:], in_=bias_bank[:, 0, 0:D_OUT].unsqueeze(1).to_broadcast([P, 4, D_OUT])
-                )
-            if n < NODE_PASSES:
-                regroup_ahat(n)
+                nc.scalar.copy(out=bias_all[:], in_=bias_bank[:, 0, 0:D_OUT])
 
         project(GRAPHS - 1)
+        aggregate(5)
         copy_y(GRAPHS - 1)
-        quantise_y(PAIRS - 1, 0)
-        quantise_y(PAIRS - 1, 1)
-        first_left = GRAPHS - CHUNK_LAG
-        for b in range(2):
-            relu_on_scalar(first_left - 1, b)
-        for chunk in range(first_left, CHUNKS):
-            aggregate(chunk)
+        relu_on_scalar(4, 0)
+        relu_on_scalar(4, 1)
+        add_bias(5, 0)
+        add_bias(5, 1)
+        aggregate(6)
+        aggregate(7)
+        relu_on_scalar(5, 0)
+        relu_on_scalar(5, 1)
+        quantise_y(4)
+        add_bias(6, 0)
+        add_bias(7, 0)
+        aggregate(8)
+        aggregate(9)
+        relu_on_scalar(6, 0)
+        relu_on_scalar(7, 0)
+        for chunk in (8, 9):
             add_bias(chunk, 0)
-            add_bias(chunk, 1)
-            for b in range(2):
-                relu_on_scalar(chunk, b)
+            relu_on_scalar(chunk, 0)

@@ -21,7 +21,7 @@ GROUPS = [(0, 1), (2, 3), (4, 5), (6,), (7,)]
 HALF = NODES // 2
 CHUNKS = [(q, half) for q in range(len(GROUPS)) for half in range(2)]
 TILES = 4
-PIECES = [(0, 0), (1, 0), (0, 1), (1, 1)]
+PIECES = [(0, 0), (0, 1), (1, 0), (1, 1)]
 CHUNK_LAG = 3
 
 FLOPS = 2 * GRAPHS * NODES * D_IN * D_OUT + 2 * GRAPHS * NODES * NODES * D_OUT
@@ -40,7 +40,7 @@ def tile_gcn_pb_kernel(tc, x, ahat, gcn1_w, gcn1_b, out):
         ctx.enter_context(tc.manual_schedule())
 
         x_sb = [keep.tile([P, NODE_PASSES, PACK, D_IN], BF16, name="x_sb%d" % g) for g in range(GRAPHS)]
-        a_raw = [keep.tile([P, PACK, HALF], BF16, name="a_raw%d" % i) for i in range(len(PIECES))]
+        a_raw = [keep.tile([P, PACK, NODES], BF16, name="a_raw%d" % c) for c in range(NODE_PASSES)]
         a_codes = keep.tile([P, NODE_PASSES, NODES], U32, align_bytes=64)
         a_scales = keep.tile([P, NODE_PASSES, NODES], U8, align_bytes=64)
         w_raw = keep.tile([P, PACK, D_OUT], BF16)
@@ -59,15 +59,13 @@ def tile_gcn_pb_kernel(tc, x, ahat, gcn1_w, gcn1_b, out):
         nc.scalar.activation(out=warm[:], in_=ones[:, 0:1], func=mybir.ActivationFunctionType.Relu)
 
         x_rows = x.rearrange("(g c p j) k -> g p c (j k)", g=GRAPHS, c=NODE_PASSES, p=P, j=PACK)
-        a_rows = ahat.rearrange("(c p j) n -> c p j n", c=NODE_PASSES, p=P, j=PACK)
+        a_rows = ahat.rearrange("(c p j) n -> c p (j n)", c=NODE_PASSES, p=P, j=PACK)
 
         def load_x(g, c):
             nc.sync.dma_start(out=x_sb[g][:, c].rearrange("p j k -> p (j k)"), in_=x_rows[g][:, c, :])
 
-        def load_ahat(piece):
-            c, half = PIECES[piece]
-            cols = slice(half * HALF, (half + 1) * HALF)
-            nc.sync.dma_start(out=a_raw[piece][:], in_=a_rows[c][:, :, cols])
+        def load_ahat(c):
+            nc.sync.dma_start(out=a_raw[c][:].rearrange("p j n -> p (j n)"), in_=a_rows[c])
 
         def load_weights():
             nc.sync.dma_start(
@@ -77,12 +75,14 @@ def tile_gcn_pb_kernel(tc, x, ahat, gcn1_w, gcn1_b, out):
             nc.sync.dma_start(out=bias_rows[0:1, :], in_=gcn1_b.rearrange("(o f) -> o f", o=1))
 
         for g in range(GRAPHS):
-            if g < len(PIECES):
-                load_ahat(g)
             for c in range(NODE_PASSES):
                 load_x(g, c)
                 if (g, c) == (0, 0):
                     load_weights()
+                if (g, c) == (0, 1):
+                    load_ahat(0)
+                if (g, c) == (2, 0):
+                    load_ahat(1)
 
         xt_banks = {}
         x_grouped = {}
@@ -159,10 +159,11 @@ def tile_gcn_pb_kernel(tc, x, ahat, gcn1_w, gcn1_b, out):
             )
 
         def regroup_ahat(piece):
+            c, half = PIECES[piece]
             a_grouped[piece] = a_stage.tile([P, 4, P, PACK], BF16, name="a_grouped", align_bytes=64)
             nc.vector.tensor_copy(
                 out=a_grouped[piece][:].rearrange("p r m j -> p m j r"),
-                in_=a_raw[piece][:].rearrange("p j (m r) -> p m j r", r=4),
+                in_=a_raw[c][:, :, half * HALF : (half + 1) * HALF].rearrange("p j (m r) -> p m j r", r=4),
             )
 
         def quantise_ahat(piece):
@@ -221,7 +222,6 @@ def tile_gcn_pb_kernel(tc, x, ahat, gcn1_w, gcn1_b, out):
             nc.scalar.activation(out=part, in_=part, func=mybir.ActivationFunctionType.Relu)
             store(chunk, b)
 
-        regroup_ahat(0)
         transpose_x(0)
         bias_bank = psum_work.tile([P, 2, 2 * D_OUT], F32, tag="bank")
         nc.tensor.matmul(out=bias_bank[:, 0, 0:D_OUT], lhsT=ones[:], rhs=bias_rows[:], start=True, stop=True)
@@ -232,16 +232,14 @@ def tile_gcn_pb_kernel(tc, x, ahat, gcn1_w, gcn1_b, out):
 
         for n in range(GRAPHS):
             chunk = n - CHUNK_LAG
-            quantise_a = 0 <= n - 1 < len(PIECES)
+            quantise_a = 0 <= n - 1 < NODE_PASSES
             if chunk >= 0 and chunk % 2 == 0:
                 quantise_y(chunk // 2)
             copy_x(n, 0)
             copy_x(n, 1)
             if quantise_a:
-                quantise_ahat(n - 1)
+                quantise_ahat(2 * (n - 1))
             quantise_x(n, 0)
-            if n + 1 < len(PIECES):
-                regroup_ahat(n + 1)
             copy_x(n, 2)
             copy_x(n, 3)
             if chunk >= 1:
@@ -254,6 +252,8 @@ def tile_gcn_pb_kernel(tc, x, ahat, gcn1_w, gcn1_b, out):
                 transpose_x(n + 1)
             if n >= 1:
                 copy_y(n - 1)
+            if quantise_a:
+                quantise_ahat(2 * (n - 1) + 1)
             quantise_x(n, 1)
             if n == GRAPHS - 1:
                 quantise_y(3)
@@ -262,6 +262,9 @@ def tile_gcn_pb_kernel(tc, x, ahat, gcn1_w, gcn1_b, out):
                 add_bias(chunk, 1)
             if n == 0:
                 nc.scalar.copy(out=bias_all[:], in_=bias_bank[:, 0, 0:D_OUT])
+            if n < NODE_PASSES:
+                regroup_ahat(2 * n)
+                regroup_ahat(2 * n + 1)
 
         project(GRAPHS - 1)
         aggregate(5)

@@ -22,6 +22,7 @@ HALF = NODES // 2
 CHUNKS = [(q, half) for q in range(len(GROUPS)) for half in range(2)]
 TILES = 4
 PIECES = [(0, 0), (0, 1), (1, 0), (1, 1)]
+EARLY = 2
 CHUNK_LAG = 3
 
 FLOPS = 2 * GRAPHS * NODES * D_IN * D_OUT + 2 * GRAPHS * NODES * NODES * D_OUT
@@ -79,10 +80,8 @@ def tile_gcn_pb_kernel(tc, x, ahat, gcn1_w, gcn1_b, out):
                 load_x(g, c)
                 if (g, c) == (0, 0):
                     load_weights()
-                if (g, c) == (0, 1):
-                    load_ahat(0)
-                if (g, c) == (2, 0):
-                    load_ahat(1)
+                if c == NODE_PASSES - 1 and g < NODE_PASSES:
+                    load_ahat(g)
 
         xt_banks = {}
         x_grouped = {}
@@ -96,9 +95,9 @@ def tile_gcn_pb_kernel(tc, x, ahat, gcn1_w, gcn1_b, out):
         o_banks = {}
         o_tiles = {}
 
-        def transpose_x(g):
+        def transpose_x(g, banks):
             words = x_sb[g][:].bitcast(F32)
-            for bank in range(4):
+            for bank in banks:
                 xt = psum_work.tile([P, 2, 2, P], F32, tag="bank")
                 xt_banks[(g, bank)] = xt
                 for t in range(2):
@@ -222,7 +221,7 @@ def tile_gcn_pb_kernel(tc, x, ahat, gcn1_w, gcn1_b, out):
             nc.scalar.activation(out=part, in_=part, func=mybir.ActivationFunctionType.Relu)
             store(chunk, b)
 
-        transpose_x(0)
+        transpose_x(0, range(4))
         bias_bank = psum_work.tile([P, 2, 2 * D_OUT], F32, tag="bank")
         nc.tensor.matmul(out=bias_bank[:, 0, 0:D_OUT], lhsT=ones[:], rhs=bias_rows[:], start=True, stop=True)
         nc.vector.tensor_copy(out=w_grouped[:], in_=w_raw[:].rearrange("q t f -> q f t"))
@@ -232,29 +231,34 @@ def tile_gcn_pb_kernel(tc, x, ahat, gcn1_w, gcn1_b, out):
 
         for n in range(GRAPHS):
             chunk = n - CHUNK_LAG
-            quantise_a = 0 <= n - 1 < NODE_PASSES
             if chunk >= 0 and chunk % 2 == 0:
                 quantise_y(chunk // 2)
             copy_x(n, 0)
             copy_x(n, 1)
-            if quantise_a:
-                quantise_ahat(2 * (n - 1))
+            if 1 <= n <= 3:
+                quantise_ahat((0, 2, 3)[n - 1])
             quantise_x(n, 0)
             copy_x(n, 2)
             copy_x(n, 3)
             if chunk >= 1:
                 relu_on_vector(chunk - 1)
-            if n >= 1:
+            if n > EARLY:
                 project(n - 1)
+            if n >= EARLY and n + 1 < GRAPHS:
+                transpose_x(n + 1, (0, 1))
             if chunk >= 0:
                 aggregate(chunk)
-            if n + 1 < GRAPHS:
-                transpose_x(n + 1)
-            if n >= 1:
+            if n >= EARLY and n + 1 < GRAPHS:
+                transpose_x(n + 1, (2, 3))
+            if n > EARLY:
                 copy_y(n - 1)
-            if quantise_a:
-                quantise_ahat(2 * (n - 1) + 1)
+            if n == 1:
+                quantise_ahat(1)
             quantise_x(n, 1)
+            if n < EARLY:
+                project(n)
+                copy_y(n)
+                transpose_x(n + 1, range(4))
             if n == GRAPHS - 1:
                 quantise_y(3)
             if chunk >= 0:

from contextlib import ExitStack

import concourse.mybir as mybir
from concourse.masks import make_identity

F32 = mybir.dt.float32
BF16 = mybir.dt.bfloat16
U32 = mybir.dt.uint32
U8 = mybir.dt.uint8
FP8X4 = mybir.dt.float8_e4m3fn_x4

P = 128
PACK = 4
K_PASS = P * PACK
GRAPHS = 8
NODES = 1024
D_IN = 512
D_OUT = 128
NODE_PASSES = NODES // K_PASS
GROUPS = [(0, 1), (2, 3), (4, 5), (6,), (7,)]
HALF = NODES // 2
CHUNKS = [(q, half) for q in range(len(GROUPS)) for half in range(2)]
TILES = 4
PIECES = [(0, 0), (0, 1), (1, 0), (1, 1)]
EARLY = 2
CHUNK_LAG = 3

FLOPS = 2 * GRAPHS * NODES * D_IN * D_OUT + 2 * GRAPHS * NODES * NODES * D_OUT


def tile_gcn_pb_kernel(tc, x, ahat, gcn1_w, gcn1_b, out):
    nc = tc.nc
    with ExitStack() as ctx:
        keep = ctx.enter_context(tc.tile_pool(name="keep", bufs=1))
        a_stage = ctx.enter_context(tc.tile_pool(name="a_stage", bufs=4))
        x_stage = ctx.enter_context(tc.tile_pool(name="x_stage", bufs=4))
        y_stage = ctx.enter_context(tc.tile_pool(name="y_stage", bufs=2))
        o_stage = ctx.enter_context(tc.tile_pool(name="o_stage", bufs=len(CHUNKS)))
        psum_y = ctx.enter_context(tc.psum_pool(name="psum_y", bufs=2))
        psum_work = ctx.enter_context(tc.psum_pool(name="psum_work", bufs=6))
        ctx.enter_context(tc.manual_schedule())

        x_sb = [keep.tile([P, NODE_PASSES, PACK, D_IN], BF16, name="x_sb%d" % g) for g in range(GRAPHS)]
        a_raw = [keep.tile([P, PACK, NODES], BF16, name="a_raw%d" % c) for c in range(NODE_PASSES)]
        a_codes = keep.tile([P, NODE_PASSES, NODES], U32, align_bytes=64)
        a_scales = keep.tile([P, NODE_PASSES, NODES], U8, align_bytes=64)
        w_raw = keep.tile([P, PACK, D_OUT], BF16)
        w_grouped = keep.tile([P, D_OUT, PACK], BF16, align_bytes=64)
        w_codes = keep.tile([P, D_OUT], U32, align_bytes=64)
        w_scales = keep.tile([P, D_OUT], U8, align_bytes=64)
        identity = keep.tile([P, P], F32)
        ones = keep.tile([P, P], BF16)
        bias_rows = keep.tile([P, D_OUT], BF16)
        bias_all = keep.tile([P, D_OUT], F32)
        warm = keep.tile([P, 1], F32)

        make_identity(nc, identity[:])
        nc.vector.memset(bias_rows[:], 0.0)
        nc.vector.memset(ones[:], 1.0)
        nc.scalar.activation(out=warm[:], in_=ones[:, 0:1], func=mybir.ActivationFunctionType.Relu)

        x_rows = x.rearrange("(g c p j) k -> g p c (j k)", g=GRAPHS, c=NODE_PASSES, p=P, j=PACK)
        a_rows = ahat.rearrange("(c p j) n -> c p (j n)", c=NODE_PASSES, p=P, j=PACK)

        def load_x(g, c):
            nc.sync.dma_start(out=x_sb[g][:, c].rearrange("p j k -> p (j k)"), in_=x_rows[g][:, c, :])

        def load_ahat(c):
            nc.sync.dma_start(out=a_raw[c][:].rearrange("p j n -> p (j n)"), in_=a_rows[c])

        def load_weights():
            nc.sync.dma_start(
                out=w_raw[:].rearrange("q (u e) f -> q u (e f)", u=2),
                in_=gcn1_w.rearrange("(u q e) f -> q u (e f)", u=2, q=P, e=2),
            )
            nc.sync.dma_start(out=bias_rows[0:1, :], in_=gcn1_b.rearrange("(o f) -> o f", o=1))

        for g in range(GRAPHS):
            for c in range(NODE_PASSES):
                load_x(g, c)
                if (g, c) == (0, 0):
                    load_weights()
                if c == NODE_PASSES - 1 and g < NODE_PASSES:
                    load_ahat(g)

        xt_banks = {}
        x_grouped = {}
        x_codes = {}
        x_scales = {}
        y_banks = {}
        y_grouped = {}
        y_codes = {}
        y_scales = {}
        a_grouped = {}
        o_banks = {}
        o_tiles = {}

        def transpose_x(g, banks):
            words = x_sb[g][:].bitcast(F32)
            for bank in banks:
                xt = psum_work.tile([P, 2, 2, P], F32, tag="bank")
                xt_banks[(g, bank)] = xt
                for t in range(2):
                    c, j = divmod(2 * bank + t, PACK)
                    for u in range(2):
                        nc.tensor.transpose(xt[:, t, u, :], words[:, c, j, u * P : (u + 1) * P], identity[:])

        def copy_x(g, bank):
            c, part = divmod(bank, 2)
            if part == 0:
                x_grouped[(g, c)] = x_stage.tile([P, PACK, P, PACK], BF16, name="x_grouped", align_bytes=64)
            nc.scalar.copy(
                out=x_grouped[(g, c)][:].bitcast(F32)[:, 2 * part : 2 * part + 2, :, :],
                in_=xt_banks[(g, bank)][:].rearrange("q t u n -> q t n u"),
            )

        def quantise_x(g, c):
            x_codes[(g, c)] = x_stage.tile([P, PACK * P], U32, name="x_codes", align_bytes=64)
            x_scales[(g, c)] = x_stage.tile([P, PACK * P], U8, name="x_scales", align_bytes=64)
            nc.vector.quantize_mx(
                out=x_codes[(g, c)][:].bitcast(FP8X4),
                scales=x_scales[(g, c)][:],
                in_=x_grouped[(g, c)][:].rearrange("q j n k -> q (j n k)"),
            )

        def project(g):
            for c in range(NODE_PASSES):
                y_bank = psum_y.tile([P, PACK, D_OUT], F32)
                y_banks[(g, c)] = y_bank
                for j in range(PACK):
                    nodes = slice(j * P, (j + 1) * P)
                    nc.tensor.matmul_mx(
                        out=y_bank[:, j, :],
                        lhsT=x_codes[(g, c)][:, nodes].bitcast(FP8X4),
                        lhsT_scale=x_scales[(g, c)][:, nodes],
                        rhs=w_codes[:].bitcast(FP8X4),
                        rhs_scale=w_scales[:],
                        start=True,
                        stop=True,
                    )

        def copy_y(g):
            q = [g in group for group in GROUPS].index(True)
            size, b = len(GROUPS[q]), GROUPS[q].index(g)
            if b == 0:
                y_grouped[q] = y_stage.tile([P, NODE_PASSES, size, D_OUT, PACK], BF16, name="y_grouped", align_bytes=64)
            for c in range(NODE_PASSES):
                nc.scalar.copy(out=y_grouped[q][:, c, b, :, :], in_=y_banks[(g, c)][:].rearrange("p j f -> p f j"))

        def quantise_y(q):
            size = len(GROUPS[q])
            y_codes[q] = y_stage.tile([P, NODE_PASSES, size * D_OUT], U32, name="y_codes", align_bytes=64)
            y_scales[q] = y_stage.tile([P, NODE_PASSES, size * D_OUT], U8, name="y_scales", align_bytes=64)
            nc.vector.quantize_mx(
                out=y_codes[q][:].rearrange("p c n -> p (c n)").bitcast(FP8X4),
                scales=y_scales[q][:].rearrange("p c n -> p (c n)"),
                in_=y_grouped[q][:].rearrange("p c b f j -> p (c b f j)"),
            )

        def regroup_ahat(piece):
            c, half = PIECES[piece]
            a_grouped[piece] = a_stage.tile([P, 4, P, PACK], BF16, name="a_grouped", align_bytes=64)
            nc.vector.tensor_copy(
                out=a_grouped[piece][:].rearrange("p r m j -> p m j r"),
                in_=a_raw[c][:, :, half * HALF : (half + 1) * HALF].rearrange("p j (m r) -> p m j r", r=4),
            )

        def quantise_ahat(piece):
            c, half = PIECES[piece]
            cols = slice(half * HALF, (half + 1) * HALF)
            nc.vector.quantize_mx(
                out=a_codes[:, c, cols].bitcast(FP8X4),
                scales=a_scales[:, c, cols],
                in_=a_grouped[piece][:].rearrange("p r m j -> p (r m j)"),
            )

        def aggregate(chunk):
            q, half = CHUNKS[chunk]
            size = len(GROUPS[q])
            for bank in range(size):
                o_bank = psum_work.tile([P, TILES // size, size * D_OUT], F32, tag="bank")
                o_banks[(chunk, bank)] = o_bank
                for t in range(TILES // size):
                    first = half * HALF + (bank * TILES // size + t) * P
                    for c in range(NODE_PASSES):
                        nc.tensor.matmul_mx(
                            out=o_bank[:, t, :],
                            lhsT=a_codes[:, c, first : first + P].bitcast(FP8X4),
                            lhsT_scale=a_scales[:, c, first : first + P],
                            rhs=y_codes[q][:, c, :].bitcast(FP8X4),
                            rhs_scale=y_scales[q][:, c, :],
                            start=(c == 0),
                            stop=(c == NODE_PASSES - 1),
                        )

        def add_bias(chunk, bank):
            size = len(GROUPS[CHUNKS[chunk][0]])
            if bank == 0:
                o_tiles[chunk] = o_stage.tile([P, size, TILES, D_OUT], F32, name="o_tile")
            first = bank * TILES // size
            nc.vector.tensor_tensor(
                out=o_tiles[chunk][:, :, first : first + TILES // size, :].rearrange("p b t f -> p t b f"),
                in0=o_banks[(chunk, bank)][:].rearrange("p t (b f) -> p t b f", b=size),
                in1=bias_all[:].unsqueeze(1).unsqueeze(1).to_broadcast([P, TILES // size, size, D_OUT]),
                op=mybir.AluOpType.add,
            )

        def store(chunk, b):
            q, half = CHUNKS[chunk]
            rows = out[GROUPS[q][b]].rearrange("(h m r) f -> h m (r f)", h=2, r=4)
            nc.sync.dma_start(out=rows[half], in_=o_tiles[chunk][:, b].rearrange("p r f -> p (r f)"))

        def relu_on_vector(chunk):
            flat = o_tiles[chunk][:].rearrange("p b r f -> p (b r f)")
            nc.vector.tensor_scalar_max(out=flat, in0=flat, scalar1=0.0)
            store(chunk, 0)
            store(chunk, 1)

        def relu_on_scalar(chunk, b):
            part = o_tiles[chunk][:, b].rearrange("p r f -> p (r f)")
            nc.scalar.activation(out=part, in_=part, func=mybir.ActivationFunctionType.Relu)
            store(chunk, b)

        transpose_x(0, range(4))
        bias_bank = psum_work.tile([P, 2, 2 * D_OUT], F32, tag="bank")
        nc.tensor.matmul(out=bias_bank[:, 0, 0:D_OUT], lhsT=ones[:], rhs=bias_rows[:], start=True, stop=True)
        nc.vector.tensor_copy(out=w_grouped[:], in_=w_raw[:].rearrange("q t f -> q f t"))
        nc.vector.quantize_mx(
            out=w_codes[:].bitcast(FP8X4), scales=w_scales[:], in_=w_grouped[:].rearrange("q f t -> q (f t)")
        )

        for n in range(GRAPHS):
            chunk = n - CHUNK_LAG
            if chunk >= 0 and chunk % 2 == 0:
                quantise_y(chunk // 2)
            copy_x(n, 0)
            copy_x(n, 1)
            if 1 <= n <= 3:
                quantise_ahat((0, 2, 3)[n - 1])
            quantise_x(n, 0)
            copy_x(n, 2)
            copy_x(n, 3)
            if chunk >= 1:
                relu_on_vector(chunk - 1)
            if n > EARLY:
                project(n - 1)
            if n >= EARLY and n + 1 < GRAPHS:
                transpose_x(n + 1, (0, 1))
            if chunk >= 0:
                aggregate(chunk)
            if n >= EARLY and n + 1 < GRAPHS:
                transpose_x(n + 1, (2, 3))
            if n > EARLY:
                copy_y(n - 1)
            if n == 1:
                quantise_ahat(1)
            quantise_x(n, 1)
            if n < EARLY:
                project(n)
                copy_y(n)
                transpose_x(n + 1, range(4))
            if n == GRAPHS - 1:
                quantise_y(3)
            if chunk >= 0:
                add_bias(chunk, 0)
                add_bias(chunk, 1)
            if n == 0:
                nc.scalar.copy(out=bias_all[:], in_=bias_bank[:, 0, 0:D_OUT])
            if n < NODE_PASSES:
                regroup_ahat(2 * n)
                regroup_ahat(2 * n + 1)

        project(GRAPHS - 1)
        aggregate(5)
        copy_y(GRAPHS - 1)
        relu_on_scalar(4, 0)
        relu_on_scalar(4, 1)
        add_bias(5, 0)
        add_bias(5, 1)
        aggregate(6)
        aggregate(7)
        relu_on_scalar(5, 0)
        relu_on_scalar(5, 1)
        quantise_y(4)
        add_bias(6, 0)
        add_bias(7, 0)
        aggregate(8)
        aggregate(9)
        relu_on_scalar(6, 0)
        relu_on_scalar(7, 0)
        for chunk in (8, 9):
            add_bias(chunk, 0)
            relu_on_scalar(chunk, 0)
